import numpy as np
import ml_dtypes


def mxq(x, axis, fmt="e4m3"):
    dtype, down = {"e4m3": (ml_dtypes.float8_e4m3fn, 7), "e5m2": (ml_dtypes.float8_e5m2, 14)}[fmt]
    v = np.moveaxis(np.asarray(x, np.float32).astype(ml_dtypes.bfloat16).astype(np.float64), axis, -1)
    blocks = v.reshape(v.shape[:-1] + (-1, 32))
    amax = np.abs(blocks).max(-1, keepdims=True)
    byte = np.maximum(np.where(amax > 0, np.frexp(amax)[1] - 1 + 127, 0) - down, 1)
    scale = np.exp2(byte - 127.0)
    codes = (blocks / scale).astype(np.float32).astype(dtype).astype(np.float64)
    return np.moveaxis((codes * scale).reshape(v.shape), -1, axis)


WIDE = False


def mx_kscale(k):
    if not WIDE:
        return np.ones(k)
    levels = np.array([30, -30])
    if k % 512:
        return np.exp2(np.random.permutation(np.resize(levels, k // 32))).repeat(32)
    a = np.empty((k // 512, 16))
    for p in range(k // 512):
        a[p, :8] = np.random.permutation(np.resize(levels, 8))
        for g in range(8):
            far = levels[np.abs(levels - a[p, g]) >= 10]
            a[p, g + 8] = far[np.random.randint(len(far))]
    return np.exp2(a.ravel()).repeat(32)


BF16 = ml_dtypes.bfloat16


def bf(x):
    return np.asarray(x, np.float32).astype(BF16)


def f64(x):
    return np.asarray(x).astype(np.float64)


E2M1 = np.array([0.0, 0.5, 1.0, 1.5, 2.0, 3.0, 4.0, 6.0, -0.0, -0.5, -1.0, -1.5, -2.0, -3.0, -4.0, -6.0])


def pack_weight(w, fmt):
    k, n = w.shape
    w = f64(bf(w)).reshape(k // 32, 32, n)
    amax = np.abs(w).max(1)
    if fmt == "e4m3":
        byte = np.frexp(amax)[1] - 1 + 127 - 7
    else:
        mant, ex = np.frexp(amax / 6.0)
        byte = np.where(mant > 0.5, ex, ex - 1) + 127
    byte = np.clip(np.where(amax > 0, byte, 1), 1, 254)
    scaled = (w * np.exp2(127.0 - byte)[:, None, :]).reshape(k, n).astype(np.float32)
    by_word = np.ascontiguousarray(scaled.reshape(k // 512, 128, 4, n).transpose(0, 1, 3, 2))
    if fmt == "e4m3":
        words = by_word.astype(ml_dtypes.float8_e4m3fn).view(np.uint8)
    else:
        c = by_word.astype(ml_dtypes.float4_e2m1fn).view(np.uint8) & 0xF
        words = c[..., 0::2] | (c[..., 1::2] << 4)
    return np.ascontiguousarray(words), np.ascontiguousarray(byte.astype(np.uint8).reshape(k // 512, 16, n))


def unpack_weight(words, scales, fmt):
    g, p, n, _ = words.shape
    if fmt == "e4m3":
        vals = np.ascontiguousarray(words).view(ml_dtypes.float8_e4m3fn).astype(np.float64)
    else:
        nib = np.empty((g, p, n, 4), np.uint8)
        nib[..., 0::2] = words & 0xF
        nib[..., 1::2] = words >> 4
        vals = E2M1[nib]
    vals = vals * np.repeat(np.exp2(scales.astype(np.float64) - 127.0), 8, axis=1)[..., None]
    return vals.transpose(0, 1, 3, 2).reshape(g * 512, n)

def pack4(w):
    words, scales = pack_weight(w, "e2m1")
    return words.reshape(words.shape[0], 128, -1), scales


def unpack4(words, scales):
    return unpack_weight(words.reshape(words.shape[0], 128, -1, 2), scales, "e2m1")


B, S, D, H, DH = 1, 512, 2048, 16, 128
E = H * DH
HALF = DH // 2
ROPE_BASE = 10000.0


def apply_rope(u):
    inv_freq = 1.0 / ROPE_BASE ** (np.arange(0, DH, 2) / DH)
    freqs = np.arange(S)[:, None] * inv_freq[None, :]
    cos = np.concatenate([np.cos(freqs), np.cos(freqs)], axis=-1)
    sin = np.concatenate([np.sin(freqs), np.sin(freqs)], axis=-1)
    rot = np.concatenate([-u[..., HALF:], u[..., :HALF]], axis=-1)
    return u * cos + rot * sin


def setup_inputs():
    s = mx_kscale(D)
    x = bf(np.random.standard_normal((B, S, D)) * s)
    wq = np.random.standard_normal((E, D)) * 0.7 / np.sqrt(D) / s[None, :]
    wk = np.random.standard_normal((E, D)) * 0.7 / np.sqrt(D) / s[None, :]
    Wq_words, Wq_scales = pack4(np.ascontiguousarray(wq.T))
    Wk_words, Wk_scales = pack4(np.ascontiguousarray(wk.T))
    return {"x": x,
            "Wq_words": Wq_words, "Wq_scales": Wq_scales,
            "Wk_words": Wk_words, "Wk_scales": Wk_scales}


def reference(x, Wq_words, Wq_scales, Wk_words, Wk_scales):
    xq = mxq(f64(x), 2, "e5m2")
    q = (xq @ unpack4(Wq_words, Wq_scales)).reshape(B, S, H, DH).transpose(0, 2, 1, 3)
    k = (xq @ unpack4(Wk_words, Wk_scales)).reshape(B, S, H, DH).transpose(0, 2, 1, 3)
    return apply_rope(q), apply_rope(k)

@@ -1,0 +1,232 @@
+import math
+from contextlib import ExitStack
+
+import concourse.mybir as mybir
+from concourse.masks import make_identity
+
+S, D, H, DH = 512, 2048, 16, 128
+HALF = DH // 2
+ROPE_BASE = 10000.0
+FLOPS = 2 * S * D * 2 * H * DH
+
+F32 = mybir.dt.float32
+BF16 = mybir.dt.bfloat16
+I32 = mybir.dt.int32
+U32 = mybir.dt.uint32
+U8 = mybir.dt.uint8
+E5M2X4 = mybir.dt.float8_e5m2_x4
+E2M1X4 = mybir.dt.float4_e2m1fn_x4
+ALU = mybir.AluOpType
+ACT = mybir.ActivationFunctionType
+
+P = 128
+PASSES = D // 512
+TILES = S // P
+N = 512
+HEADS = N // DH
+CHUNKS = 2 * H // HEADS
+RADIX = 8
+PLANES = 4
+
+
+def tile_multiheadattention_pa_kernel(tc, x, Wq_words, Wq_scales, Wk_words, Wk_scales, out_0, out_1):
+    nc = tc.nc
+    x_rows = x[0].rearrange("(p t) k -> p t k", t=TILES)
+    words_hbm = (Wq_words, Wk_words)
+    scales_hbm = (Wq_scales, Wk_scales)
+    outs = [o[0].rearrange("h (p t) c -> p h t c", t=TILES) for o in (out_0, out_1)]
+    per_proj = CHUNKS // 2
+
+    with ExitStack() as ctx:
+        keep = ctx.enter_context(tc.tile_pool(name="keep", bufs=1))
+        work = ctx.enter_context(tc.tile_pool(name="work", bufs=3))
+        psum_t = ctx.enter_context(tc.psum_pool(name="psum_t", bufs=3))
+        psum_a = ctx.enter_context(tc.psum_pool(name="psum_a", bufs=5))
+        ctx.enter_context(tc.manual_schedule())
+
+        ident = keep.tile([P, P], F32, name="ident")
+        pos = keep.tile([P, TILES], I32, name="pos")
+        turns = keep.tile([P, HALF, TILES], F32, name="turns")
+        whole = keep.tile([P, 2, HALF * TILES], I32, name="whole")
+        frac = keep.tile([P, 2, HALF, TILES], F32, name="frac")
+        table = keep.tile([P, TILES, 4, HALF], F32, name="table")
+        planes = [keep.tile([P, PASSES, N], U8, name="plane%d" % i, align_bytes=64) for i in range(PLANES)]
+        x_raw = {}
+        x_codes = {}
+        x_scales = {}
+        w_words = {}
+        rotated = {}
+
+        def load_x(t, half):
+            x_raw[t, half] = keep.tile([P, D // 2], BF16, name="x%d_%d" % (t, half))
+            nc.sync.dma_start(out=x_raw[t, half][:], in_=x_rows[:, t, half * (D // 2):(half + 1) * (D // 2)])
+
+        def load_x_whole(t):
+            both = keep.tile([P, 2, D // 2], BF16, name="x%d" % t)
+            nc.sync.dma_start(out=both[:].rearrange("p a k -> p (a k)"), in_=x_rows[:, t, :])
+            for half in range(2):
+                x_raw[t, half] = both[:, half, :]
+
+        def load_words(first, count):
+            tile = keep.tile([P, PASSES, count * 2 * N], U8, name="w%d" % first, align_bytes=64)
+            proj, c = divmod(first, per_proj)
+            src = words_hbm[proj][:, :, c * 2 * N:(c + count) * 2 * N].rearrange("g p n -> p g n")
+            nc.sync.dma_start(out=tile[:].bitcast(I32), in_=src.bitcast(I32))
+            for i in range(count):
+                for g in range(PASSES):
+                    w_words[first + i, g] = tile[:, g, i * 2 * N:(i + 1) * 2 * N]
+
+        def load_words_half(c, half):
+            tile = keep.tile([P, 2, 2 * N], U8, name="w%d_%d" % (c, half), align_bytes=64)
+            src = words_hbm[0][2 * half:2 * half + 2, :, c * 2 * N:(c + 1) * 2 * N].rearrange("g p n -> p g n")
+            nc.sync.dma_start(out=tile[:].bitcast(I32), in_=src.bitcast(I32))
+            for g in range(2):
+                w_words[c, 2 * half + g] = tile[:, g, :]
+
+        def load_scales(c):
+            proj, cc = divmod(c, per_proj)
+            for r in range(4):
+                src = scales_hbm[proj][:, r:16:4, cc * N:(cc + 1) * N].rearrange("g q n -> q g n")
+                nc.sync.dma_start(out=planes[c % PLANES][r:P:32, :, :].bitcast(I32), in_=src.bitcast(I32))
+
+        def transpose_half(t, half):
+            words = x_raw[t, half][:].bitcast(F32)
+            bank = psum_t.tile([P, 2, 2, P], F32, name="bank_t")
+            for g in range(2):
+                for u in range(2):
+                    nc.tensor.transpose(bank[:, g, u, :], words[:, 256 * g + u:256 * (g + 1):2], ident[:])
+            return bank
+
+        def interleave(bank):
+            grouped = work.tile([P, 2 * P * 4], BF16, name="grouped", align_bytes=64)
+            nc.scalar.copy(out=grouped[:].bitcast(F32).rearrange("p (g r u) -> p g r u", g=2, u=2),
+                           in_=bank[:].rearrange("p g u r -> p g r u"))
+            return grouped
+
+        def quantize(t, half, grouped):
+            x_codes[t, half] = keep.tile([P, 2 * P], U32, name="xc%d_%d" % (t, half), align_bytes=64)
+            x_scales[t, half] = keep.tile([P, 2 * P], U8, name="xs%d_%d" % (t, half), align_bytes=64)
+            nc.vector.quantize_mx(out=x_codes[t, half][:].bitcast(E5M2X4), scales=x_scales[t, half][:], in_=grouped[:])
+
+        def prepare(t):
+            staged = [interleave(transpose_half(t, half)) for half in range(2)]
+            return staged
+
+        def quantize_tile(t, staged):
+            for half in range(2):
+                quantize(t, half, staged[half])
+
+        def project(c, t):
+            acc = psum_a.tile([P, N], F32, name="acc")
+            for g in range(PASSES):
+                half, gg = divmod(g, 2)
+                nc.tensor.matmul_mx(
+                    out=acc[:],
+                    lhsT=x_codes[t, half][:, gg * P:(gg + 1) * P].bitcast(E5M2X4),
+                    lhsT_scale=x_scales[t, half][:, gg * P:(gg + 1) * P],
+                    rhs=w_words[c, g].bitcast(E2M1X4),
+                    rhs_scale=planes[c % PLANES][:, g, :],
+                    start=(g == 0), stop=(g == PASSES - 1))
+            return acc
+
+        def multiply(acc, t, terms):
+            shape = [P, HEADS, 2, 2, HALF]
+            nc.vector.tensor_tensor(
+                out=terms.rearrange("p h a (b j) -> p h a b j", b=2),
+                in0=acc[:].rearrange("p (h a j) -> p h a j", a=2, j=HALF).unsqueeze(3).to_broadcast(shape),
+                in1=table[:, t].rearrange("p (a b) j -> p a b j", a=2).unsqueeze(1).to_broadcast(shape),
+                op=ALU.mult)
+
+        def staging(c):
+            if c not in rotated:
+                rotated[c] = work.tile([P, HEADS, TILES, DH], F32, name="rotated")
+            return rotated[c]
+
+        def rotate(c, tiles, engine):
+            terms = work.tile([P, len(tiles), HEADS, 2, DH], F32, name="terms", bufs=4)
+            for i, t in enumerate(tiles):
+                multiply(project(c, t), t, terms[:, i])
+            dst = staging(c)[:, :, tiles[0]:tiles[-1] + 1, :].rearrange("p h t c -> p t h c")
+            engine.tensor_tensor(out=dst, in0=terms[:, :, :, 0, :], in1=terms[:, :, :, 1, :], op=ALU.add)
+
+        def store(c, t0, t1):
+            proj, cc = divmod(c, per_proj)
+            nc.sync.dma_start(out=outs[proj][:, cc * HEADS:(cc + 1) * HEADS, t0:t1, :], in_=rotated[c][:, :, t0:t1, :])
+
+        def sines(t0, t1):
+            count = t1 - t0
+            f_sin = frac[:, 0, :, t0:t1].rearrange("p j t -> p t j")
+            f_cos = frac[:, 1, :, t0:t1].rearrange("p j t -> p t j").unsqueeze(2).to_broadcast([P, count, 2, HALF])
+            nc.scalar.activation(out=table[:, t0:t1, 0:4:3, :], in_=f_cos, func=ACT.Sin, scale=2 * math.pi)
+            nc.scalar.activation(out=table[:, t0:t1, 1, :], in_=f_sin, func=ACT.Sin, scale=2 * math.pi)
+            nc.scalar.activation(out=table[:, t0:t1, 2, :], in_=f_sin, func=ACT.Sin, scale=-2 * math.pi)
+
+        nc.gpsimd.iota(pos[:], [[1, TILES]], base=0, channel_multiplier=TILES)
+        make_identity(nc, ident[:])
+        nc.vector.memset(planes[0][:].bitcast(I32), 0)
+        load_x(0, 0)
+        load_x(0, 1)
+        load_scales(0)
+        load_words_half(0, 0)
+        load_words_half(0, 1)
+        load_x_whole(1)
+        nc.vector.memset(planes[1][:].bitcast(I32), 0)
+        load_scales(1)
+        load_words(1, 1)
+        load_x_whole(2)
+        load_x_whole(3)
+        step = ROPE_BASE ** (-1.0 / HALF)
+        for j in range(RADIX):
+            nc.vector.tensor_scalar(out=turns[:, j, :], in0=pos[:], scalar1=step ** j / (2 * math.pi), scalar2=None, op0=ALU.mult)
+        nc.vector.memset(planes[2][:].bitcast(I32), 0)
+        for a in range(1, HALF // RADIX):
+            nc.vector.tensor_scalar(out=turns[:, a * RADIX:(a + 1) * RADIX, :], in0=turns[:, 0:RADIX, :],
+                                    scalar1=step ** (a * RADIX), scalar2=None, op0=ALU.mult)
+        nc.vector.memset(planes[3][:].bitcast(I32), 0)
+        flat = turns[:].rearrange("p j t -> p (j t)")
+        for i, shift in enumerate((0.0, 0.25)):
+            nc.vector.tensor_scalar(out=whole[:, i, :], in0=flat, scalar1=shift, scalar2=None, op0=ALU.add)
+        for i, shift in enumerate((0.0, 0.25)):
+            nc.vector.scalar_tensor_tensor(out=frac[:, i].rearrange("p j t -> p (j t)"), in0=flat, scalar=shift,
+                                           in1=whole[:, i, :], op0=ALU.add, op1=ALU.subtract)
+        load_words(2, 2)
+        load_scales(2)
+        load_scales(3)
+        load_words(4, 2)
+        load_words(6, 2)
+
+        sines(0, 1)
+        quantize_tile(0, prepare(0))
+        sines(1, TILES)
+        rotate(0, [0], nc.gpsimd)
+        quantize_tile(1, prepare(1))
+        rotate(1, [0], nc.gpsimd)
+        quantize_tile(2, prepare(2))
+        staged = prepare(3)
+        rotate(0, [1], nc.gpsimd)
+        quantize_tile(3, staged)
+        rotate(1, [1], nc.gpsimd)
+        for t in (2, 3):
+            rotate(0, [t], nc.gpsimd)
+            rotate(1, [t], nc.gpsimd)
+        load_scales(4)
+        load_scales(5)
+        store(0, 0, TILES)
+        store(1, 0, TILES)
+        last = CHUNKS - 1
+        for c in range(2, last):
+            rotate(c, [0, 1], nc.gpsimd)
+            if c == last - 1:
+                store(c, 0, 2)
+            rotate(c, [2, 3], nc.gpsimd)
+            if c == 3:
+                load_scales(6)
+                load_scales(7)
+            store(c, 2 if c == last - 1 else 0, TILES)
+        terms = keep.tile([P, TILES, HEADS, 2, DH], F32, name="terms_last")
+        for t in range(TILES):
+            multiply(project(last, t), t, terms[:, t])
+        for h in range(HEADS):
+            done = keep.tile([P, TILES, DH], F32, name="done%d" % h)
+            nc.vector.tensor_tensor(out=done[:], in0=terms[:, :, h, 0, :], in1=terms[:, :, h, 1, :], op=ALU.add)
+            nc.sync.dma_start(out=outs[1][:, H - HEADS + h, :, :], in_=done[:])

@@ -142,12 +142,18 @@ def tile_multiheadattention_pa_kernel(tc, x, Wq_words, Wq_scales, Wk_words, Wk_s
                 rotated[c] = work.tile([P, HEADS, TILES, DH], F32, name="rotated")
             return rotated[c]
 
-        def rotate(c, tiles, engine):
+        def products(c, tiles):
             terms = work.tile([P, len(tiles), HEADS, 2, DH], F32, name="terms", bufs=4)
             for i, t in enumerate(tiles):
                 multiply(project(c, t), t, terms[:, i])
+            return terms
+
+        def add_halves(c, tiles, terms, engine):
             dst = staging(c)[:, :, tiles[0]:tiles[-1] + 1, :].rearrange("p h t c -> p t h c")
             engine.tensor_tensor(out=dst, in0=terms[:, :, :, 0, :], in1=terms[:, :, :, 1, :], op=ALU.add)
+
+        def rotate(c, tiles):
+            add_halves(c, tiles, products(c, tiles), nc.gpsimd)
 
         def store(c, t0, t1):
             proj, cc = divmod(c, per_proj)
@@ -166,29 +172,29 @@ def tile_multiheadattention_pa_kernel(tc, x, Wq_words, Wq_scales, Wk_words, Wk_s
         nc.vector.memset(planes[0][:].bitcast(I32), 0)
         load_x(0, 0)
         load_x(0, 1)
+        load_x_whole(1)
         load_scales(0)
         load_words_half(0, 0)
         load_words_half(0, 1)
-        load_x_whole(1)
-        nc.vector.memset(planes[1][:].bitcast(I32), 0)
-        load_scales(1)
-        load_words(1, 1)
         load_x_whole(2)
         load_x_whole(3)
         step = ROPE_BASE ** (-1.0 / HALF)
         for j in range(RADIX):
             nc.vector.tensor_scalar(out=turns[:, j, :], in0=pos[:], scalar1=step ** j / (2 * math.pi), scalar2=None, op0=ALU.mult)
-        nc.vector.memset(planes[2][:].bitcast(I32), 0)
+        nc.vector.memset(planes[1][:].bitcast(I32), 0)
         for a in range(1, HALF // RADIX):
             nc.vector.tensor_scalar(out=turns[:, a * RADIX:(a + 1) * RADIX, :], in0=turns[:, 0:RADIX, :],
                                     scalar1=step ** (a * RADIX), scalar2=None, op0=ALU.mult)
-        nc.vector.memset(planes[3][:].bitcast(I32), 0)
+        nc.vector.memset(planes[2][:].bitcast(I32), 0)
         flat = turns[:].rearrange("p j t -> p (j t)")
         for i, shift in enumerate((0.0, 0.25)):
             nc.vector.tensor_scalar(out=whole[:, i, :], in0=flat, scalar1=shift, scalar2=None, op0=ALU.add)
         for i, shift in enumerate((0.0, 0.25)):
             nc.vector.scalar_tensor_tensor(out=frac[:, i].rearrange("p j t -> p (j t)"), in0=flat, scalar=shift,
                                            in1=whole[:, i, :], op0=ALU.add, op1=ALU.subtract)
+        nc.vector.memset(planes[3][:].bitcast(I32), 0)
+        load_scales(1)
+        load_words(1, 1)
         load_words(2, 2)
         load_scales(2)
         load_scales(3)
@@ -197,31 +203,22 @@ def tile_multiheadattention_pa_kernel(tc, x, Wq_words, Wq_scales, Wk_words, Wk_s
 
         sines(0, 1)
         quantize_tile(0, prepare(0))
-        sines(1, TILES)
-        rotate(0, [0], nc.gpsimd)
         quantize_tile(1, prepare(1))
-        rotate(1, [0], nc.gpsimd)
-        quantize_tile(2, prepare(2))
-        staged = prepare(3)
-        rotate(0, [1], nc.gpsimd)
-        quantize_tile(3, staged)
-        rotate(1, [1], nc.gpsimd)
-        for t in (2, 3):
-            rotate(0, [t], nc.gpsimd)
-            rotate(1, [t], nc.gpsimd)
-        load_scales(4)
-        load_scales(5)
-        store(0, 0, TILES)
-        store(1, 0, TILES)
+        sines(1, TILES)
+        first = [products(0, [t]) for t in range(2)]
+        for t in range(2):
+            staged = prepare(2 + t)
+            add_halves(0, [t], first[t], nc.vector)
+            quantize_tile(2 + t, staged)
         last = CHUNKS - 1
-        for c in range(2, last):
-            rotate(c, [0, 1], nc.gpsimd)
+        for c in range(last):
+            if c > 0:
+                rotate(c, [0, 1])
             if c == last - 1:
                 store(c, 0, 2)
-            rotate(c, [2, 3], nc.gpsimd)
-            if c == 3:
-                load_scales(6)
-                load_scales(7)
+            rotate(c, [2, 3])
+            if c < CHUNKS - PLANES:
+                load_scales(c + PLANES)
             store(c, 2 if c == last - 1 else 0, TILES)
         terms = keep.tile([P, TILES, HEADS, 2, DH], F32, name="terms_last")
         for t in range(TILES):

import math
from contextlib import ExitStack

import concourse.mybir as mybir
from concourse.masks import make_identity

S, D, H, DH = 512, 2048, 16, 128
HALF = DH // 2
ROPE_BASE = 10000.0
FLOPS = 2 * S * D * 2 * H * DH

F32 = mybir.dt.float32
BF16 = mybir.dt.bfloat16
I32 = mybir.dt.int32
U32 = mybir.dt.uint32
U8 = mybir.dt.uint8
E5M2X4 = mybir.dt.float8_e5m2_x4
E2M1X4 = mybir.dt.float4_e2m1fn_x4
ALU = mybir.AluOpType
ACT = mybir.ActivationFunctionType

P = 128
PASSES = D // 512
TILES = S // P
N = 512
HEADS = N // DH
CHUNKS = 2 * H // HEADS
RADIX = 8
PLANES = 4


def tile_multiheadattention_pa_kernel(tc, x, Wq_words, Wq_scales, Wk_words, Wk_scales, out_0, out_1):
    nc = tc.nc
    x_rows = x[0].rearrange("(p t) k -> p t k", t=TILES)
    words_hbm = (Wq_words, Wk_words)
    scales_hbm = (Wq_scales, Wk_scales)
    outs = [o[0].rearrange("h (p t) c -> p h t c", t=TILES) for o in (out_0, out_1)]
    per_proj = CHUNKS // 2

    with ExitStack() as ctx:
        keep = ctx.enter_context(tc.tile_pool(name="keep", bufs=1))
        work = ctx.enter_context(tc.tile_pool(name="work", bufs=3))
        psum_t = ctx.enter_context(tc.psum_pool(name="psum_t", bufs=3))
        psum_a = ctx.enter_context(tc.psum_pool(name="psum_a", bufs=5))
        ctx.enter_context(tc.manual_schedule())

        ident = keep.tile([P, P], F32, name="ident")
        pos = keep.tile([P, TILES], I32, name="pos")
        turns = keep.tile([P, HALF, TILES], F32, name="turns")
        whole = keep.tile([P, 2, HALF * TILES], I32, name="whole")
        frac = keep.tile([P, 2, HALF, TILES], F32, name="frac")
        table = keep.tile([P, TILES, 4, HALF], F32, name="table")
        planes = [keep.tile([P, PASSES, N], U8, name="plane%d" % i, align_bytes=64) for i in range(PLANES)]
        x_raw = {}
        x_codes = {}
        x_scales = {}
        w_words = {}
        rotated = {}

        def load_x(t, half):
            x_raw[t, half] = keep.tile([P, D // 2], BF16, name="x%d_%d" % (t, half))
            nc.sync.dma_start(out=x_raw[t, half][:], in_=x_rows[:, t, half * (D // 2):(half + 1) * (D // 2)])

        def load_x_whole(t):
            both = keep.tile([P, 2, D // 2], BF16, name="x%d" % t)
            nc.sync.dma_start(out=both[:].rearrange("p a k -> p (a k)"), in_=x_rows[:, t, :])
            for half in range(2):
                x_raw[t, half] = both[:, half, :]

        def load_words(first, count):
            tile = keep.tile([P, PASSES, count * 2 * N], U8, name="w%d" % first, align_bytes=64)
            proj, c = divmod(first, per_proj)
            src = words_hbm[proj][:, :, c * 2 * N:(c + count) * 2 * N].rearrange("g p n -> p g n")
            nc.sync.dma_start(out=tile[:].bitcast(I32), in_=src.bitcast(I32))
            for i in range(count):
                for g in range(PASSES):
                    w_words[first + i, g] = tile[:, g, i * 2 * N:(i + 1) * 2 * N]

        def load_words_half(c, half):
            tile = keep.tile([P, 2, 2 * N], U8, name="w%d_%d" % (c, half), align_bytes=64)
            src = words_hbm[0][2 * half:2 * half + 2, :, c * 2 * N:(c + 1) * 2 * N].rearrange("g p n -> p g n")
            nc.sync.dma_start(out=tile[:].bitcast(I32), in_=src.bitcast(I32))
            for g in range(2):
                w_words[c, 2 * half + g] = tile[:, g, :]

        def load_scales(c):
            proj, cc = divmod(c, per_proj)
            for r in range(4):
                src = scales_hbm[proj][:, r:16:4, cc * N:(cc + 1) * N].rearrange("g q n -> q g n")
                nc.sync.dma_start(out=planes[c % PLANES][r:P:32, :, :].bitcast(I32), in_=src.bitcast(I32))

        def transpose_half(t, half):
            words = x_raw[t, half][:].bitcast(F32)
            bank = psum_t.tile([P, 2, 2, P], F32, name="bank_t")
            for g in range(2):
                for u in range(2):
                    nc.tensor.transpose(bank[:, g, u, :], words[:, 256 * g + u:256 * (g + 1):2], ident[:])
            return bank

        def interleave(bank):
            grouped = work.tile([P, 2 * P * 4], BF16, name="grouped", align_bytes=64)
            nc.scalar.copy(out=grouped[:].bitcast(F32).rearrange("p (g r u) -> p g r u", g=2, u=2),
                           in_=bank[:].rearrange("p g u r -> p g r u"))
            return grouped

        def quantize(t, half, grouped):
            x_codes[t, half] = keep.tile([P, 2 * P], U32, name="xc%d_%d" % (t, half), align_bytes=64)
            x_scales[t, half] = keep.tile([P, 2 * P], U8, name="xs%d_%d" % (t, half), align_bytes=64)
            nc.vector.quantize_mx(out=x_codes[t, half][:].bitcast(E5M2X4), scales=x_scales[t, half][:], in_=grouped[:])

        def prepare(t):
            staged = [interleave(transpose_half(t, half)) for half in range(2)]
            return staged

        def quantize_tile(t, staged):
            for half in range(2):
                quantize(t, half, staged[half])

        def project(c, t):
            acc = psum_a.tile([P, N], F32, name="acc")
            for g in range(PASSES):
                half, gg = divmod(g, 2)
                nc.tensor.matmul_mx(
                    out=acc[:],
                    lhsT=x_codes[t, half][:, gg * P:(gg + 1) * P].bitcast(E5M2X4),
                    lhsT_scale=x_scales[t, half][:, gg * P:(gg + 1) * P],
                    rhs=w_words[c, g].bitcast(E2M1X4),
                    rhs_scale=planes[c % PLANES][:, g, :],
                    start=(g == 0), stop=(g == PASSES - 1))
            return acc

        def multiply(acc, t, terms):
            shape = [P, HEADS, 2, 2, HALF]
            nc.vector.tensor_tensor(
                out=terms.rearrange("p h a (b j) -> p h a b j", b=2),
                in0=acc[:].rearrange("p (h a j) -> p h a j", a=2, j=HALF).unsqueeze(3).to_broadcast(shape),
                in1=table[:, t].rearrange("p (a b) j -> p a b j", a=2).unsqueeze(1).to_broadcast(shape),
                op=ALU.mult)

        def staging(c):
            if c not in rotated:
                rotated[c] = work.tile([P, HEADS, TILES, DH], F32, name="rotated")
            return rotated[c]

        def products(c, tiles):
            terms = work.tile([P, len(tiles), HEADS, 2, DH], F32, name="terms", bufs=4)
            for i, t in enumerate(tiles):
                multiply(project(c, t), t, terms[:, i])
            return terms

        def add_halves(c, tiles, terms, engine):
            dst = staging(c)[:, :, tiles[0]:tiles[-1] + 1, :].rearrange("p h t c -> p t h c")
            engine.tensor_tensor(out=dst, in0=terms[:, :, :, 0, :], in1=terms[:, :, :, 1, :], op=ALU.add)

        def rotate(c, tiles):
            add_halves(c, tiles, products(c, tiles), nc.gpsimd)

        def store(c, t0, t1):
            proj, cc = divmod(c, per_proj)
            nc.sync.dma_start(out=outs[proj][:, cc * HEADS:(cc + 1) * HEADS, t0:t1, :], in_=rotated[c][:, :, t0:t1, :])

        def sines(t0, t1):
            count = t1 - t0
            f_sin = frac[:, 0, :, t0:t1].rearrange("p j t -> p t j")
            f_cos = frac[:, 1, :, t0:t1].rearrange("p j t -> p t j").unsqueeze(2).to_broadcast([P, count, 2, HALF])
            nc.scalar.activation(out=table[:, t0:t1, 0:4:3, :], in_=f_cos, func=ACT.Sin, scale=2 * math.pi)
            nc.scalar.activation(out=table[:, t0:t1, 1, :], in_=f_sin, func=ACT.Sin, scale=2 * math.pi)
            nc.scalar.activation(out=table[:, t0:t1, 2, :], in_=f_sin, func=ACT.Sin, scale=-2 * math.pi)

        nc.gpsimd.iota(pos[:], [[1, TILES]], base=0, channel_multiplier=TILES)
        make_identity(nc, ident[:])
        nc.vector.memset(planes[0][:].bitcast(I32), 0)
        load_x(0, 0)
        load_x(0, 1)
        load_x_whole(1)
        load_scales(0)
        load_words_half(0, 0)
        load_words_half(0, 1)
        load_x_whole(2)
        load_x_whole(3)
        step = ROPE_BASE ** (-1.0 / HALF)
        for j in range(RADIX):
            nc.vector.tensor_scalar(out=turns[:, j, :], in0=pos[:], scalar1=step ** j / (2 * math.pi), scalar2=None, op0=ALU.mult)
        nc.vector.memset(planes[1][:].bitcast(I32), 0)
        for a in range(1, HALF // RADIX):
            nc.vector.tensor_scalar(out=turns[:, a * RADIX:(a + 1) * RADIX, :], in0=turns[:, 0:RADIX, :],
                                    scalar1=step ** (a * RADIX), scalar2=None, op0=ALU.mult)
        nc.vector.memset(planes[2][:].bitcast(I32), 0)
        flat = turns[:].rearrange("p j t -> p (j t)")
        for i, shift in enumerate((0.0, 0.25)):
            nc.vector.tensor_scalar(out=whole[:, i, :], in0=flat, scalar1=shift, scalar2=None, op0=ALU.add)
        for i, shift in enumerate((0.0, 0.25)):
            nc.vector.scalar_tensor_tensor(out=frac[:, i].rearrange("p j t -> p (j t)"), in0=flat, scalar=shift,
                                           in1=whole[:, i, :], op0=ALU.add, op1=ALU.subtract)
        nc.vector.memset(planes[3][:].bitcast(I32), 0)
        load_scales(1)
        load_words(1, 1)
        load_words(2, 2)
        load_scales(2)
        load_scales(3)
        load_words(4, 2)
        load_words(6, 2)

        sines(0, 1)
        quantize_tile(0, prepare(0))
        quantize_tile(1, prepare(1))
        sines(1, TILES)
        first = [products(0, [t]) for t in range(2)]
        for t in range(2):
            staged = prepare(2 + t)
            add_halves(0, [t], first[t], nc.vector)
            quantize_tile(2 + t, staged)
        last = CHUNKS - 1
        for c in range(last):
            if c > 0:
                rotate(c, [0, 1])
            if c == last - 1:
                store(c, 0, 2)
            rotate(c, [2, 3])
            if c < CHUNKS - PLANES:
                load_scales(c + PLANES)
            store(c, 2 if c == last - 1 else 0, TILES)
        terms = keep.tile([P, TILES, HEADS, 2, DH], F32, name="terms_last")
        for t in range(TILES):
            multiply(project(last, t), t, terms[:, t])
        for h in range(HEADS):
            done = keep.tile([P, TILES, DH], F32, name="done%d" % h)
            nc.vector.tensor_tensor(out=done[:], in0=terms[:, :, h, 0, :], in1=terms[:, :, h, 1, :], op=ALU.add)
            nc.sync.dma_start(out=outs[1][:, H - HEADS + h, :, :], in_=done[:])
